import numpy as np
import ml_dtypes


def mxq(x, axis, fmt="e4m3"):
    dtype, down = {"e4m3": (ml_dtypes.float8_e4m3fn, 7), "e5m2": (ml_dtypes.float8_e5m2, 14)}[fmt]
    v = np.moveaxis(np.asarray(x, np.float32).astype(ml_dtypes.bfloat16).astype(np.float64), axis, -1)
    blocks = v.reshape(v.shape[:-1] + (-1, 32))
    amax = np.abs(blocks).max(-1, keepdims=True)
    byte = np.maximum(np.where(amax > 0, np.frexp(amax)[1] - 1 + 127, 0) - down, 1)
    scale = np.exp2(byte - 127.0)
    codes = (blocks / scale).astype(np.float32).astype(dtype).astype(np.float64)
    return np.moveaxis((codes * scale).reshape(v.shape), -1, axis)


WIDE = False


def mx_kscale(k):
    if not WIDE:
        return np.ones(k)
    levels = np.array([10, -10, 5, -5, 0])
    a = np.random.permutation(np.resize(levels, k // 512 * 4)).reshape(k // 512, 4)
    idx = np.arange(k)
    return np.exp2(a[idx // 512, idx % 128 // 32])


BF16 = ml_dtypes.bfloat16


def bf(x):
    return np.asarray(x, np.float32).astype(BF16)


def f64(x):
    return np.asarray(x).astype(np.float64)


B, C_IN, H, W, N_HID, N_CLS = 1024, 3, 32, 32, 1024, 128
D = C_IN * H * W
EPS = 1e-12
BN_EPS = 1e-5


def unit_rows(v):
    return v / (np.sqrt((v * v).sum(axis=1, keepdims=True)) + EPS)


def batchnorm(c, gamma, beta):
    mu = c.mean(axis=0)
    var = c.var(axis=0)
    return (c - mu) * (1.0 / np.sqrt(var + BN_EPS)) * gamma + beta


def setup_inputs():
    s = mx_kscale(D)
    r = np.sqrt(np.mean(s * s) * np.mean(1.0 / (s * s)))
    v = (0.5 - 0.5 / np.pi) / D
    comp = np.exp2(np.round(np.log2(r * np.sqrt((v / (r * r) + BN_EPS) / (v + BN_EPS)))))
    contrast = np.exp2(np.random.uniform(-1.0, 1.0, B))[:, None, None, None]
    length = np.exp2(np.random.uniform(-3.0, 0.0, N_HID))[:, None]
    return {"x": bf(np.random.standard_normal((B, C_IN, H, W)) * contrast * s.reshape(C_IN, H, W)),
            "w1": bf(np.random.standard_normal((N_HID, D)) * length / np.sqrt(D) / s[None, :]),
            "g1": bf((1.0 + 0.1 * np.random.standard_normal(N_HID)) * comp),
            "b1": bf(0.1 * np.random.standard_normal(N_HID))}


def reference(x, w1, g1, b1):
    xf = f64(x).reshape(B, -1)
    xn = unit_rows(xf)
    wn = unit_rows(f64(w1))
    c = np.clip(mxq(xn, 1, "e4m3") @ mxq(wn, 1, "e4m3").T, 0.0, 1.0)
    return batchnorm(c, f64(g1), f64(b1))

@@ -1,0 +1,267 @@
+from contextlib import ExitStack
+
+import concourse.masks as masks
+import concourse.mybir as mybir
+
+F32 = mybir.dt.float32
+BF16 = mybir.dt.bfloat16
+U32 = mybir.dt.uint32
+U8 = mybir.dt.uint8
+FP8X4 = mybir.dt.float8_e4m3fn_x4
+ALU = mybir.AluOpType
+ACT = mybir.ActivationFunctionType
+
+P = 128
+PACK = 4
+K_PASS = P * PACK
+BATCH = 1024
+HIDDEN = 1024
+DEPTH = 3072
+PASSES = DEPTH // K_PASS
+X_TILES = BATCH // P
+W_TILES = HIDDEN // P
+ROW_TILES = X_TILES + W_TILES
+PER_BANK = 4
+BANKS = DEPTH // 2 // (P * PER_BANK)
+N_MOVE = 512
+HALVES = BATCH // N_MOVE
+EPS = 1e-12
+BN_EPS = 1e-5
+LOADS_AHEAD = 6
+
+FLOPS = 2 * BATCH * HIDDEN * DEPTH
+
+
+def tile_net_pa_kernel(tc, x, w1, g1, b1, out):
+    nc = tc.nc
+    x_tiles = x.rearrange("(i p) c h w -> i p (c h w)", p=P)
+    w_tiles = w1.rearrange("(i p) k -> i p k", p=P)
+    rows_in_dram = [x_tiles[i] for i in range(X_TILES)] + [w_tiles[j] for j in range(W_TILES)]
+    out_tiles = out.rearrange("(t p) (j n) -> j p t n", p=P, n=P)
+
+    with ExitStack() as ctx:
+        const = ctx.enter_context(tc.tile_pool(name="const", bufs=1))
+        raw_pool = ctx.enter_context(tc.tile_pool(name="raw", bufs=LOADS_AHEAD + 2))
+        squares_pool = ctx.enter_context(tc.tile_pool(name="squares", bufs=2))
+        unit_pool = ctx.enter_context(tc.tile_pool(name="unit", bufs=2))
+        grouped_pool = ctx.enter_context(tc.tile_pool(name="grouped", bufs=2))
+        weight_pool = ctx.enter_context(tc.tile_pool(name="weight", bufs=3))
+        small = ctx.enter_context(tc.tile_pool(name="small", bufs=4))
+        sim_pool = ctx.enter_context(tc.tile_pool(name="sim", bufs=3))
+        normed_pool = ctx.enter_context(tc.tile_pool(name="normed", bufs=2))
+        result_pool = ctx.enter_context(tc.tile_pool(name="result", bufs=3))
+        turn_in_pool = ctx.enter_context(tc.psum_pool(name="turn_in", bufs=4))
+        turn_out_pool = ctx.enter_context(tc.psum_pool(name="turn_out", bufs=2))
+        acc_pool = ctx.enter_context(tc.psum_pool(name="acc", bufs=2))
+        ctx.enter_context(tc.manual_schedule())
+
+        one = const.tile([P, 1], F32)
+        nc.vector.memset(one[:], 1.0)
+        warm = const.tile([P, 1], F32)
+        nc.scalar.sqrt(warm[:], one[:])
+
+        ident_f32 = const.tile([P, P], F32)
+        nc.vector.memset(ident_f32[:], 0.0)
+        masks.make_identity(nc, ident_f32[:], nomemset=True)
+
+        x_codes = const.tile([P, PASSES, BATCH], U32, align_bytes=64)
+        x_scales = const.tile([P, PASSES, BATCH], U8, align_bytes=64)
+
+        raw, norm, unit, turned_in, grouped = {}, {}, {}, {}, {}
+        weights, sums, sims, moments, deviations, normeds, turned_out = {}, {}, {}, {}, {}, {}, {}
+
+        vector_rows = const.tile([P, P], BF16)
+        gain_shift = const.tile([P, 2 * W_TILES], F32)
+
+        def load_gain_and_shift():
+            nc.vector.memset(vector_rows[:], 0.0)
+            nc.sync.dma_start(out=vector_rows[0:W_TILES, :], in_=g1.rearrange("(j n) -> j n", n=P))
+            nc.sync.dma_start(
+                out=vector_rows[W_TILES : 2 * W_TILES, :], in_=b1.rearrange("(j n) -> j n", n=P)
+            )
+
+        def spread_gain_and_shift():
+            ident_bf16 = const.tile([P, P], BF16)
+            nc.vector.tensor_copy(out=ident_bf16[:], in_=ident_f32[:])
+            vector_cols = turn_out_pool.tile([P, P], BF16, tag="turned_back")
+            nc.tensor.transpose(vector_cols[:], vector_rows[:], ident_bf16[:])
+            nc.vector.tensor_copy(out=gain_shift[:], in_=vector_cols[:, 0 : 2 * W_TILES])
+
+        def load(r):
+            rows = raw_pool.tile([P, DEPTH], BF16)
+            nc.sync.dma_start(out=rows[:], in_=rows_in_dram[r])
+            raw[r] = rows
+
+        def measure(r):
+            squares = squares_pool.tile([P, DEPTH], BF16)
+            sum_squares = small.tile([P, 1], F32)
+            nc.scalar.activation(
+                out=squares[:], in_=raw[r][:], func=ACT.Square, accum_out=sum_squares[:]
+            )
+            length = small.tile([P, 1], F32)
+            nc.scalar.sqrt(length[:], sum_squares[:])
+            norm[r] = length
+
+        def scale(r):
+            padded = small.tile([P, 1], F32)
+            nc.vector.tensor_scalar_add(out=padded[:], in0=norm[r][:], scalar1=EPS)
+            inverse = small.tile([P, 1], F32)
+            nc.vector.reciprocal(out=inverse[:], in_=padded[:])
+            scaled = unit_pool.tile([P, DEPTH], BF16)
+            nc.vector.tensor_scalar_mul(out=scaled[:], in0=raw[r][:], scalar1=inverse[:, 0:1])
+            unit[r] = scaled
+
+        def turn(r):
+            pairs = unit[r][:].bitcast(F32)
+            turned_in[r] = []
+            for m in range(BANKS):
+                turned = turn_in_pool.tile([P, PER_BANK, P], F32)
+                for q in range(PER_BANK):
+                    first = (PER_BANK * m + q) * P
+                    nc.tensor.transpose(turned[:, q, :], pairs[:, first : first + P], ident_f32[:])
+                turned_in[r].append(turned)
+
+        def regroup(r):
+            lined = grouped_pool.tile([P, DEPTH], BF16, align_bytes=64)
+            lined_pairs = lined[:].bitcast(F32).rearrange("p (g c u) -> p g c u", g=PASSES, u=2)
+            for m in range(BANKS):
+                source = turned_in[r][m][:].rearrange("p (g u) c -> p g c u", u=2)
+                target = lined_pairs[:, 2 * m : 2 * m + 2, :, :]
+                if r >= X_TILES and m > 0:
+                    nc.scalar.copy(out=target, in_=source)
+                else:
+                    nc.vector.tensor_copy(out=target, in_=source)
+            grouped[r] = lined
+
+        def quantise(r):
+            if r < X_TILES:
+                cols = slice(r * P, (r + 1) * P)
+                for g in range(PASSES):
+                    nc.vector.quantize_mx(
+                        out=x_codes[:, g, cols].bitcast(FP8X4),
+                        scales=x_scales[:, g, cols],
+                        in_=grouped[r][:, g * K_PASS : (g + 1) * K_PASS],
+                    )
+            else:
+                w_codes = weight_pool.tile([P, PASSES * P], U32, align_bytes=64)
+                w_scales = weight_pool.tile([P, PASSES * P], U8, align_bytes=64)
+                for first, width in ((0, 4 * P), (4 * P, 2 * P)):
+                    nc.vector.quantize_mx(
+                        out=w_codes[:, first : first + width].bitcast(FP8X4),
+                        scales=w_scales[:, first : first + width],
+                        in_=grouped[r][:, PACK * first : PACK * (first + width)],
+                    )
+                weights[r - X_TILES] = (w_codes, w_scales)
+
+        def multiply(j):
+            w_codes, w_scales = weights[j]
+            sums[j] = []
+            for h in range(HALVES):
+                half = slice(h * N_MOVE, (h + 1) * N_MOVE)
+                acc = acc_pool.tile([P, N_MOVE], F32)
+                for g in range(PASSES):
+                    w_cols = slice(g * P, (g + 1) * P)
+                    nc.tensor.matmul_mx(
+                        out=acc[:],
+                        lhsT=w_codes[:, w_cols].bitcast(FP8X4),
+                        lhsT_scale=w_scales[:, w_cols],
+                        rhs=x_codes[:, g, half].bitcast(FP8X4),
+                        rhs_scale=x_scales[:, g, half],
+                        start=(g == 0),
+                        stop=(g == PASSES - 1),
+                    )
+                sums[j].append(acc)
+
+        def clip_and_count(j):
+            sim = sim_pool.tile([P, BATCH], F32)
+            stats = small.tile([P, HALVES, 6], F32)
+            for h in range(HALVES):
+                half = slice(h * N_MOVE, (h + 1) * N_MOVE)
+                nc.vector.tensor_scalar(
+                    out=sim[:, half], in0=sums[j][h][:], scalar1=0.0, scalar2=1.0,
+                    op0=ALU.max, op1=ALU.min,
+                )
+                nc.vector.bn_stats(out=stats[:, h, :], in_=sim[:, half])
+            mean_var = small.tile([P, 2], F32)
+            nc.vector.bn_aggr(out=mean_var[:], in_=stats[:].rearrange("p h s -> p (h s)"))
+            padded_var = small.tile([P, 1], F32)
+            nc.vector.tensor_scalar_add(out=padded_var[:], in0=mean_var[:, 1:2], scalar1=BN_EPS)
+            sims[j] = sim
+            moments[j] = (mean_var, padded_var)
+
+        def deviation(j):
+            std = small.tile([P, 1], F32)
+            nc.scalar.sqrt(std[:], moments[j][1][:])
+            deviations[j] = std
+
+        def normalise(j):
+            inverse_std = small.tile([P, 1], F32)
+            nc.vector.reciprocal(out=inverse_std[:], in_=deviations[j][:])
+            slope = small.tile([P, 1], F32)
+            nc.vector.tensor_mul(out=slope[:], in0=inverse_std[:], in1=gain_shift[:, j : j + 1])
+            drop = small.tile([P, 1], F32)
+            nc.vector.tensor_scalar(
+                out=drop[:], in0=moments[j][0][:, 0:1], scalar1=slope[:, 0:1],
+                scalar2=gain_shift[:, W_TILES + j : W_TILES + j + 1],
+                op0=ALU.mult, op1=ALU.subtract,
+            )
+            normed = normed_pool.tile([P, BATCH], F32)
+            nc.vector.tensor_scalar(
+                out=normed[:], in0=sims[j][:], scalar1=slope[:, 0:1], scalar2=drop[:, 0:1],
+                op0=ALU.mult, op1=ALU.subtract,
+            )
+            normeds[j] = normed
+
+        def turn_back(j):
+            turned_out[j] = []
+            for m in range(X_TILES // PER_BANK):
+                turned_back = turn_out_pool.tile([P, PER_BANK, P], F32)
+                for q in range(PER_BANK):
+                    t = PER_BANK * m + q
+                    nc.tensor.transpose(
+                        turned_back[:, q, :], normeds[j][:, t * P : (t + 1) * P], ident_f32[:]
+                    )
+                turned_out[j].append(turned_back)
+
+        def store(j):
+            result = result_pool.tile([P, X_TILES, P], F32)
+            for m in range(X_TILES // PER_BANK):
+                nc.scalar.copy(
+                    out=result[:, PER_BANK * m : PER_BANK * (m + 1), :], in_=turned_out[j][m][:]
+                )
+            nc.sync.dma_start(out=out_tiles[j], in_=result[:])
+
+        for r in range(LOADS_AHEAD):
+            load(r)
+        load_gain_and_shift()
+        for step in range(ROW_TILES + 4):
+            scaled_now = step - 1
+            grouped_now = step - 2
+            multiplied_now = step - 3 - X_TILES
+            stored_now = step - 4 - X_TILES
+            if 0 <= grouped_now < ROW_TILES:
+                regroup(grouped_now)
+            if 0 <= multiplied_now < W_TILES:
+                multiply(multiplied_now)
+            if 0 <= stored_now < W_TILES:
+                normalise(stored_now)
+            if step < ROW_TILES:
+                measure(step)
+            if 0 <= scaled_now < ROW_TILES:
+                scale(scaled_now)
+            if 0 <= stored_now < W_TILES:
+                turn_back(stored_now)
+            if 0 <= scaled_now < ROW_TILES:
+                turn(scaled_now)
+            if 0 <= multiplied_now < W_TILES:
+                clip_and_count(multiplied_now)
+            if 0 <= stored_now < W_TILES:
+                store(stored_now)
+            if 0 <= multiplied_now < W_TILES:
+                deviation(multiplied_now)
+            if 0 <= grouped_now < ROW_TILES:
+                quantise(grouped_now)
+            if step + LOADS_AHEAD < ROW_TILES:
+                load(step + LOADS_AHEAD)
+            if step == X_TILES:
+                spread_gain_and_shift()

@@ -43,8 +43,8 @@ def tile_net_pa_kernel(tc, x, w1, g1, b1, out):
         const = ctx.enter_context(tc.tile_pool(name="const", bufs=1))
         raw_pool = ctx.enter_context(tc.tile_pool(name="raw", bufs=LOADS_AHEAD + 2))
         squares_pool = ctx.enter_context(tc.tile_pool(name="squares", bufs=2))
-        unit_pool = ctx.enter_context(tc.tile_pool(name="unit", bufs=2))
-        grouped_pool = ctx.enter_context(tc.tile_pool(name="grouped", bufs=2))
+        unit_pool = ctx.enter_context(tc.tile_pool(name="unit", bufs=3))
+        grouped_pool = ctx.enter_context(tc.tile_pool(name="grouped", bufs=3))
         weight_pool = ctx.enter_context(tc.tile_pool(name="weight", bufs=3))
         small = ctx.enter_context(tc.tile_pool(name="small", bufs=4))
         sim_pool = ctx.enter_context(tc.tile_pool(name="sim", bufs=3))
@@ -53,12 +53,13 @@ def tile_net_pa_kernel(tc, x, w1, g1, b1, out):
         turn_in_pool = ctx.enter_context(tc.psum_pool(name="turn_in", bufs=4))
         turn_out_pool = ctx.enter_context(tc.psum_pool(name="turn_out", bufs=2))
         acc_pool = ctx.enter_context(tc.psum_pool(name="acc", bufs=2))
-        ctx.enter_context(tc.manual_schedule())
 
-        one = const.tile([P, 1], F32)
-        nc.vector.memset(one[:], 1.0)
-        warm = const.tile([P, 1], F32)
-        nc.scalar.sqrt(warm[:], one[:])
+        power_half = const.tile([P, 1], F32)
+        nc.vector.memset(power_half[:], 0.5)
+        power_minus_half = const.tile([P, 1], F32)
+        nc.vector.memset(power_minus_half[:], -0.5)
+        power_minus_one = const.tile([P, 1], F32)
+        nc.vector.memset(power_minus_one[:], -1.0)
 
         ident_f32 = const.tile([P, P], F32)
         nc.vector.memset(ident_f32[:], 0.0)
@@ -68,7 +69,7 @@ def tile_net_pa_kernel(tc, x, w1, g1, b1, out):
         x_scales = const.tile([P, PASSES, BATCH], U8, align_bytes=64)
 
         raw, norm, unit, turned_in, grouped = {}, {}, {}, {}, {}
-        weights, sums, sims, moments, deviations, normeds, turned_out = {}, {}, {}, {}, {}, {}, {}
+        weights, sums, sims, lines, normeds, turned_out = {}, {}, {}, {}, {}, {}
 
         vector_rows = const.tile([P, P], BF16)
         gain_shift = const.tile([P, 2 * W_TILES], F32)
@@ -85,7 +86,12 @@ def tile_net_pa_kernel(tc, x, w1, g1, b1, out):
             nc.vector.tensor_copy(out=ident_bf16[:], in_=ident_f32[:])
             vector_cols = turn_out_pool.tile([P, P], BF16, tag="turned_back")
             nc.tensor.transpose(vector_cols[:], vector_rows[:], ident_bf16[:])
-            nc.vector.tensor_copy(out=gain_shift[:], in_=vector_cols[:, 0 : 2 * W_TILES])
+            nc.vector.tensor_copy(out=gain_shift[:, 0:W_TILES], in_=vector_cols[:, 0:W_TILES])
+            nc.vector.tensor_scalar_mul(
+                out=gain_shift[:, W_TILES : 2 * W_TILES],
+                in0=vector_cols[:, W_TILES : 2 * W_TILES],
+                scalar1=-1.0,
+            )
 
         def load(r):
             rows = raw_pool.tile([P, DEPTH], BF16)
@@ -99,16 +105,20 @@ def tile_net_pa_kernel(tc, x, w1, g1, b1, out):
                 out=squares[:], in_=raw[r][:], func=ACT.Square, accum_out=sum_squares[:]
             )
             length = small.tile([P, 1], F32)
-            nc.scalar.sqrt(length[:], sum_squares[:])
-            norm[r] = length
+            nc.gpsimd.tensor_tensor(out=length[:], in0=sum_squares[:], in1=power_half[:], op=ALU.pow)
+            padded = small.tile([P, 1], F32)
+            nc.gpsimd.tensor_scalar(
+                out=padded[:], in0=length[:], scalar1=EPS, scalar2=1.0, op0=ALU.add, op1=ALU.mult
+            )
+            inverse = small.tile([P, 1], F32)
+            nc.gpsimd.tensor_tensor(
+                out=inverse[:], in0=padded[:], in1=power_minus_one[:], op=ALU.pow
+            )
+            norm[r] = inverse
 
         def scale(r):
-            padded = small.tile([P, 1], F32)
-            nc.vector.tensor_scalar_add(out=padded[:], in0=norm[r][:], scalar1=EPS)
-            inverse = small.tile([P, 1], F32)
-            nc.vector.reciprocal(out=inverse[:], in_=padded[:])
             scaled = unit_pool.tile([P, DEPTH], BF16)
-            nc.vector.tensor_scalar_mul(out=scaled[:], in0=raw[r][:], scalar1=inverse[:, 0:1])
+            nc.vector.tensor_scalar_mul(out=scaled[:], in0=raw[r][:], scalar1=norm[r][:, 0:1])
             unit[r] = scaled
 
         def turn(r):
@@ -172,39 +182,45 @@ def tile_net_pa_kernel(tc, x, w1, g1, b1, out):
                     )
                 sums[j].append(acc)
 
-        def clip_and_count(j):
-            sim = sim_pool.tile([P, BATCH], F32)
+        def clip(j, h):
+            if h == 0:
+                sim = sim_pool.tile([P, BATCH], F32)
+                sims[j] = sim
+            half_cols = slice(h * N_MOVE, (h + 1) * N_MOVE)
+            nc.vector.tensor_scalar(
+                out=sims[j][:, half_cols], in0=sums[j][h][:], scalar1=0.0, scalar2=1.0,
+                op0=ALU.max, op1=ALU.min,
+            )
+
+        def count(j):
             stats = small.tile([P, HALVES, 6], F32)
             for h in range(HALVES):
-                half = slice(h * N_MOVE, (h + 1) * N_MOVE)
-                nc.vector.tensor_scalar(
-                    out=sim[:, half], in0=sums[j][h][:], scalar1=0.0, scalar2=1.0,
-                    op0=ALU.max, op1=ALU.min,
-                )
-                nc.vector.bn_stats(out=stats[:, h, :], in_=sim[:, half])
+                nc.vector.bn_stats(out=stats[:, h, :], in_=sims[j][:, h * N_MOVE : (h + 1) * N_MOVE])
             mean_var = small.tile([P, 2], F32)
             nc.vector.bn_aggr(out=mean_var[:], in_=stats[:].rearrange("p h s -> p (h s)"))
             padded_var = small.tile([P, 1], F32)
-            nc.vector.tensor_scalar_add(out=padded_var[:], in0=mean_var[:, 1:2], scalar1=BN_EPS)
-            sims[j] = sim
-            moments[j] = (mean_var, padded_var)
-
-        def deviation(j):
-            std = small.tile([P, 1], F32)
-            nc.scalar.sqrt(std[:], moments[j][1][:])
-            deviations[j] = std
+            nc.gpsimd.tensor_scalar(
+                out=padded_var[:], in0=mean_var[:, 1:2], scalar1=BN_EPS, scalar2=1.0,
+                op0=ALU.add, op1=ALU.mult,
+            )
+            inverse_std = small.tile([P, 1], F32)
+            nc.gpsimd.tensor_tensor(
+                out=inverse_std[:], in0=padded_var[:], in1=power_minus_half[:], op=ALU.pow
+            )
+            slope = small.tile([P, 1], F32)
+            nc.gpsimd.tensor_tensor(
+                out=slope[:], in0=inverse_std[:], in1=gain_shift[:, j : j + 1], op=ALU.mult
+            )
+            drop = small.tile([P, 1], F32)
+            nc.gpsimd.tensor_scalar(
+                out=drop[:], in0=mean_var[:, 0:1], scalar1=slope[:, 0:1],
+                scalar2=gain_shift[:, W_TILES + j : W_TILES + j + 1],
+                op0=ALU.mult, op1=ALU.add,
+            )
+            lines[j] = (slope, drop)
 
         def normalise(j):
-            inverse_std = small.tile([P, 1], F32)
-            nc.vector.reciprocal(out=inverse_std[:], in_=deviations[j][:])
-            slope = small.tile([P, 1], F32)
-            nc.vector.tensor_mul(out=slope[:], in0=inverse_std[:], in1=gain_shift[:, j : j + 1])
-            drop = small.tile([P, 1], F32)
-            nc.vector.tensor_scalar(
-                out=drop[:], in0=moments[j][0][:, 0:1], scalar1=slope[:, 0:1],
-                scalar2=gain_shift[:, W_TILES + j : W_TILES + j + 1],
-                op0=ALU.mult, op1=ALU.subtract,
-            )
+            slope, drop = lines[j]
             normed = normed_pool.tile([P, BATCH], F32)
             nc.vector.tensor_scalar(
                 out=normed[:], in0=sims[j][:], scalar1=slope[:, 0:1], scalar2=drop[:, 0:1],
@@ -254,13 +270,14 @@ def tile_net_pa_kernel(tc, x, w1, g1, b1, out):
             if 0 <= scaled_now < ROW_TILES:
                 turn(scaled_now)
             if 0 <= multiplied_now < W_TILES:
-                clip_and_count(multiplied_now)
-            if 0 <= stored_now < W_TILES:
-                store(stored_now)
-            if 0 <= multiplied_now < W_TILES:
-                deviation(multiplied_now)
+                clip(multiplied_now, 0)
             if 0 <= grouped_now < ROW_TILES:
                 quantise(grouped_now)
+            if 0 <= multiplied_now < W_TILES:
+                clip(multiplied_now, 1)
+                count(multiplied_now)
+            if 0 <= stored_now < W_TILES:
+                store(stored_now)
             if step + LOADS_AHEAD < ROW_TILES:
                 load(step + LOADS_AHEAD)
             if step == X_TILES:

@@ -53,6 +53,7 @@ def tile_net_pa_kernel(tc, x, w1, g1, b1, out):
         turn_in_pool = ctx.enter_context(tc.psum_pool(name="turn_in", bufs=4))
         turn_out_pool = ctx.enter_context(tc.psum_pool(name="turn_out", bufs=2))
         acc_pool = ctx.enter_context(tc.psum_pool(name="acc", bufs=2))
+        ctx.enter_context(tc.manual_schedule())
 
         power_half = const.tile([P, 1], F32)
         nc.vector.memset(power_half[:], 0.5)
@@ -69,7 +70,7 @@ def tile_net_pa_kernel(tc, x, w1, g1, b1, out):
         x_scales = const.tile([P, PASSES, BATCH], U8, align_bytes=64)
 
         raw, norm, unit, turned_in, grouped = {}, {}, {}, {}, {}
-        weights, sums, sims, lines, normeds, turned_out = {}, {}, {}, {}, {}, {}
+        weights, sums, sims, counts, lines, normeds, turned_out = {}, {}, {}, {}, {}, {}, {}
 
         vector_rows = const.tile([P, P], BF16)
         gain_shift = const.tile([P, 2 * W_TILES], F32)
@@ -192,12 +193,17 @@ def tile_net_pa_kernel(tc, x, w1, g1, b1, out):
                 op0=ALU.max, op1=ALU.min,
             )
 
-        def count(j):
-            stats = small.tile([P, HALVES, 6], F32)
-            for h in range(HALVES):
-                nc.vector.bn_stats(out=stats[:, h, :], in_=sims[j][:, h * N_MOVE : (h + 1) * N_MOVE])
+        def count(j, h):
+            if h == 0:
+                stats = small.tile([P, HALVES, 6], F32)
+                counts[j] = stats
+            nc.vector.bn_stats(
+                out=counts[j][:, h, :], in_=sims[j][:, h * N_MOVE : (h + 1) * N_MOVE]
+            )
+
+        def fit(j):
             mean_var = small.tile([P, 2], F32)
-            nc.vector.bn_aggr(out=mean_var[:], in_=stats[:].rearrange("p h s -> p (h s)"))
+            nc.vector.bn_aggr(out=mean_var[:], in_=counts[j][:].rearrange("p h s -> p (h s)"))
             padded_var = small.tile([P, 1], F32)
             nc.gpsimd.tensor_scalar(
                 out=padded_var[:], in0=mean_var[:, 1:2], scalar1=BN_EPS, scalar2=1.0,
@@ -250,22 +256,26 @@ def tile_net_pa_kernel(tc, x, w1, g1, b1, out):
         for r in range(LOADS_AHEAD):
             load(r)
         load_gain_and_shift()
-        for step in range(ROW_TILES + 4):
+        for step in range(ROW_TILES + 6):
             scaled_now = step - 1
             grouped_now = step - 2
             multiplied_now = step - 3 - X_TILES
-            stored_now = step - 4 - X_TILES
-            if 0 <= grouped_now < ROW_TILES:
-                regroup(grouped_now)
+            fitted_now = step - 4 - X_TILES
+            stored_now = step - 5 - X_TILES
             if 0 <= multiplied_now < W_TILES:
                 multiply(multiplied_now)
-            if 0 <= stored_now < W_TILES:
-                normalise(stored_now)
-            if step < ROW_TILES:
-                measure(step)
+            if 0 <= grouped_now < ROW_TILES:
+                regroup(grouped_now)
+            if 0 <= fitted_now < W_TILES:
+                count(fitted_now, 1)
             if 0 <= scaled_now < ROW_TILES:
                 scale(scaled_now)
+            if 0 <= fitted_now < W_TILES:
+                fit(fitted_now)
+            if step < ROW_TILES:
+                measure(step)
             if 0 <= stored_now < W_TILES:
+                normalise(stored_now)
                 turn_back(stored_now)
             if 0 <= scaled_now < ROW_TILES:
                 turn(scaled_now)
@@ -275,7 +285,7 @@ def tile_net_pa_kernel(tc, x, w1, g1, b1, out):
                 quantise(grouped_now)
             if 0 <= multiplied_now < W_TILES:
                 clip(multiplied_now, 1)
-                count(multiplied_now)
+                count(multiplied_now, 0)
             if 0 <= stored_now < W_TILES:
                 store(stored_now)
             if step + LOADS_AHEAD < ROW_TILES:

@@ -28,6 +28,7 @@ HALVES = BATCH // N_MOVE
 EPS = 1e-12
 BN_EPS = 1e-5
 LOADS_AHEAD = 6
+FIRST_SHARED = X_TILES + 2
 
 FLOPS = 2 * BATCH * HIDDEN * DEPTH
 
@@ -49,7 +50,7 @@ def tile_net_pa_kernel(tc, x, w1, g1, b1, out):
         small = ctx.enter_context(tc.tile_pool(name="small", bufs=4))
         sim_pool = ctx.enter_context(tc.tile_pool(name="sim", bufs=3))
         normed_pool = ctx.enter_context(tc.tile_pool(name="normed", bufs=2))
-        result_pool = ctx.enter_context(tc.tile_pool(name="result", bufs=3))
+        result_pool = ctx.enter_context(tc.tile_pool(name="result", bufs=6))
         turn_in_pool = ctx.enter_context(tc.psum_pool(name="turn_in", bufs=4))
         turn_out_pool = ctx.enter_context(tc.psum_pool(name="turn_out", bufs=2))
         acc_pool = ctx.enter_context(tc.psum_pool(name="acc", bufs=2))
@@ -138,7 +139,7 @@ def tile_net_pa_kernel(tc, x, w1, g1, b1, out):
             for m in range(BANKS):
                 source = turned_in[r][m][:].rearrange("p (g u) c -> p g c u", u=2)
                 target = lined_pairs[:, 2 * m : 2 * m + 2, :, :]
-                if r >= X_TILES and m > 0:
+                if r >= FIRST_SHARED and m > 0:
                     nc.scalar.copy(out=target, in_=source)
                 else:
                     nc.vector.tensor_copy(out=target, in_=source)
@@ -228,10 +229,13 @@ def tile_net_pa_kernel(tc, x, w1, g1, b1, out):
         def normalise(j):
             slope, drop = lines[j]
             normed = normed_pool.tile([P, BATCH], F32)
-            nc.vector.tensor_scalar(
-                out=normed[:], in0=sims[j][:], scalar1=slope[:, 0:1], scalar2=drop[:, 0:1],
-                op0=ALU.mult, op1=ALU.subtract,
-            )
+            for h in range(HALVES):
+                half_cols = slice(h * N_MOVE, (h + 1) * N_MOVE)
+                nc.vector.tensor_scalar(
+                    out=normed[:, half_cols], in0=sims[j][:, half_cols],
+                    scalar1=slope[:, 0:1], scalar2=drop[:, 0:1],
+                    op0=ALU.mult, op1=ALU.subtract,
+                )
             normeds[j] = normed
 
         def turn_back(j):
@@ -246,12 +250,12 @@ def tile_net_pa_kernel(tc, x, w1, g1, b1, out):
                 turned_out[j].append(turned_back)
 
         def store(j):
-            result = result_pool.tile([P, X_TILES, P], F32)
             for m in range(X_TILES // PER_BANK):
-                nc.scalar.copy(
-                    out=result[:, PER_BANK * m : PER_BANK * (m + 1), :], in_=turned_out[j][m][:]
+                result = result_pool.tile([P, PER_BANK, P], F32)
+                nc.scalar.copy(out=result[:], in_=turned_out[j][m][:])
+                nc.sync.dma_start(
+                    out=out_tiles[j][:, PER_BANK * m : PER_BANK * (m + 1), :], in_=result[:]
                 )
-            nc.sync.dma_start(out=out_tiles[j], in_=result[:])
 
         for r in range(LOADS_AHEAD):
             load(r)
@@ -264,12 +268,10 @@ def tile_net_pa_kernel(tc, x, w1, g1, b1, out):
             stored_now = step - 5 - X_TILES
             if 0 <= multiplied_now < W_TILES:
                 multiply(multiplied_now)
-            if 0 <= grouped_now < ROW_TILES:
-                regroup(grouped_now)
             if 0 <= fitted_now < W_TILES:
                 count(fitted_now, 1)
-            if 0 <= scaled_now < ROW_TILES:
-                scale(scaled_now)
+            if 0 <= grouped_now < ROW_TILES:
+                regroup(grouped_now)
             if 0 <= fitted_now < W_TILES:
                 fit(fitted_now)
             if step < ROW_TILES:
@@ -278,6 +280,7 @@ def tile_net_pa_kernel(tc, x, w1, g1, b1, out):
                 normalise(stored_now)
                 turn_back(stored_now)
             if 0 <= scaled_now < ROW_TILES:
+                scale(scaled_now)
                 turn(scaled_now)
             if 0 <= multiplied_now < W_TILES:
                 clip(multiplied_now, 0)

@@ -270,17 +270,16 @@ def tile_net_pa_kernel(tc, x, w1, g1, b1, out):
                 multiply(multiplied_now)
             if 0 <= fitted_now < W_TILES:
                 count(fitted_now, 1)
-            if 0 <= grouped_now < ROW_TILES:
-                regroup(grouped_now)
-            if 0 <= fitted_now < W_TILES:
-                fit(fitted_now)
-            if step < ROW_TILES:
-                measure(step)
             if 0 <= stored_now < W_TILES:
                 normalise(stored_now)
                 turn_back(stored_now)
+            if 0 <= fitted_now < W_TILES:
+                fit(fitted_now)
             if 0 <= scaled_now < ROW_TILES:
                 scale(scaled_now)
+            if 0 <= grouped_now < ROW_TILES:
+                regroup(grouped_now)
+            if 0 <= scaled_now < ROW_TILES:
                 turn(scaled_now)
             if 0 <= multiplied_now < W_TILES:
                 clip(multiplied_now, 0)
@@ -288,6 +287,9 @@ def tile_net_pa_kernel(tc, x, w1, g1, b1, out):
                 quantise(grouped_now)
             if 0 <= multiplied_now < W_TILES:
                 clip(multiplied_now, 1)
+            if step < ROW_TILES:
+                measure(step)
+            if 0 <= multiplied_now < W_TILES:
                 count(multiplied_now, 0)
             if 0 <= stored_now < W_TILES:
                 store(stored_now)

from contextlib import ExitStack

import concourse.masks as masks
import concourse.mybir as mybir

F32 = mybir.dt.float32
BF16 = mybir.dt.bfloat16
U32 = mybir.dt.uint32
U8 = mybir.dt.uint8
FP8X4 = mybir.dt.float8_e4m3fn_x4
ALU = mybir.AluOpType
ACT = mybir.ActivationFunctionType

P = 128
PACK = 4
K_PASS = P * PACK
BATCH = 1024
HIDDEN = 1024
DEPTH = 3072
PASSES = DEPTH // K_PASS
X_TILES = BATCH // P
W_TILES = HIDDEN // P
ROW_TILES = X_TILES + W_TILES
PER_BANK = 4
BANKS = DEPTH // 2 // (P * PER_BANK)
N_MOVE = 512
HALVES = BATCH // N_MOVE
EPS = 1e-12
BN_EPS = 1e-5
LOADS_AHEAD = 6
FIRST_SHARED = X_TILES + 2

FLOPS = 2 * BATCH * HIDDEN * DEPTH


def tile_net_pa_kernel(tc, x, w1, g1, b1, out):
    nc = tc.nc
    x_tiles = x.rearrange("(i p) c h w -> i p (c h w)", p=P)
    w_tiles = w1.rearrange("(i p) k -> i p k", p=P)
    rows_in_dram = [x_tiles[i] for i in range(X_TILES)] + [w_tiles[j] for j in range(W_TILES)]
    out_tiles = out.rearrange("(t p) (j n) -> j p t n", p=P, n=P)

    with ExitStack() as ctx:
        const = ctx.enter_context(tc.tile_pool(name="const", bufs=1))
        raw_pool = ctx.enter_context(tc.tile_pool(name="raw", bufs=LOADS_AHEAD + 2))
        squares_pool = ctx.enter_context(tc.tile_pool(name="squares", bufs=2))
        unit_pool = ctx.enter_context(tc.tile_pool(name="unit", bufs=3))
        grouped_pool = ctx.enter_context(tc.tile_pool(name="grouped", bufs=3))
        weight_pool = ctx.enter_context(tc.tile_pool(name="weight", bufs=3))
        small = ctx.enter_context(tc.tile_pool(name="small", bufs=4))
        sim_pool = ctx.enter_context(tc.tile_pool(name="sim", bufs=3))
        normed_pool = ctx.enter_context(tc.tile_pool(name="normed", bufs=2))
        result_pool = ctx.enter_context(tc.tile_pool(name="result", bufs=6))
        turn_in_pool = ctx.enter_context(tc.psum_pool(name="turn_in", bufs=4))
        turn_out_pool = ctx.enter_context(tc.psum_pool(name="turn_out", bufs=2))
        acc_pool = ctx.enter_context(tc.psum_pool(name="acc", bufs=2))
        ctx.enter_context(tc.manual_schedule())

        power_half = const.tile([P, 1], F32)
        nc.vector.memset(power_half[:], 0.5)
        power_minus_half = const.tile([P, 1], F32)
        nc.vector.memset(power_minus_half[:], -0.5)
        power_minus_one = const.tile([P, 1], F32)
        nc.vector.memset(power_minus_one[:], -1.0)

        ident_f32 = const.tile([P, P], F32)
        nc.vector.memset(ident_f32[:], 0.0)
        masks.make_identity(nc, ident_f32[:], nomemset=True)

        x_codes = const.tile([P, PASSES, BATCH], U32, align_bytes=64)
        x_scales = const.tile([P, PASSES, BATCH], U8, align_bytes=64)

        raw, norm, unit, turned_in, grouped = {}, {}, {}, {}, {}
        weights, sums, sims, counts, lines, normeds, turned_out = {}, {}, {}, {}, {}, {}, {}

        vector_rows = const.tile([P, P], BF16)
        gain_shift = const.tile([P, 2 * W_TILES], F32)

        def load_gain_and_shift():
            nc.vector.memset(vector_rows[:], 0.0)
            nc.sync.dma_start(out=vector_rows[0:W_TILES, :], in_=g1.rearrange("(j n) -> j n", n=P))
            nc.sync.dma_start(
                out=vector_rows[W_TILES : 2 * W_TILES, :], in_=b1.rearrange("(j n) -> j n", n=P)
            )

        def spread_gain_and_shift():
            ident_bf16 = const.tile([P, P], BF16)
            nc.vector.tensor_copy(out=ident_bf16[:], in_=ident_f32[:])
            vector_cols = turn_out_pool.tile([P, P], BF16, tag="turned_back")
            nc.tensor.transpose(vector_cols[:], vector_rows[:], ident_bf16[:])
            nc.vector.tensor_copy(out=gain_shift[:, 0:W_TILES], in_=vector_cols[:, 0:W_TILES])
            nc.vector.tensor_scalar_mul(
                out=gain_shift[:, W_TILES : 2 * W_TILES],
                in0=vector_cols[:, W_TILES : 2 * W_TILES],
                scalar1=-1.0,
            )

        def load(r):
            rows = raw_pool.tile([P, DEPTH], BF16)
            nc.sync.dma_start(out=rows[:], in_=rows_in_dram[r])
            raw[r] = rows

        def measure(r):
            squares = squares_pool.tile([P, DEPTH], BF16)
            sum_squares = small.tile([P, 1], F32)
            nc.scalar.activation(
                out=squares[:], in_=raw[r][:], func=ACT.Square, accum_out=sum_squares[:]
            )
            length = small.tile([P, 1], F32)
            nc.gpsimd.tensor_tensor(out=length[:], in0=sum_squares[:], in1=power_half[:], op=ALU.pow)
            padded = small.tile([P, 1], F32)
            nc.gpsimd.tensor_scalar(
                out=padded[:], in0=length[:], scalar1=EPS, scalar2=1.0, op0=ALU.add, op1=ALU.mult
            )
            inverse = small.tile([P, 1], F32)
            nc.gpsimd.tensor_tensor(
                out=inverse[:], in0=padded[:], in1=power_minus_one[:], op=ALU.pow
            )
            norm[r] = inverse

        def scale(r):
            scaled = unit_pool.tile([P, DEPTH], BF16)
            nc.vector.tensor_scalar_mul(out=scaled[:], in0=raw[r][:], scalar1=norm[r][:, 0:1])
            unit[r] = scaled

        def turn(r):
            pairs = unit[r][:].bitcast(F32)
            turned_in[r] = []
            for m in range(BANKS):
                turned = turn_in_pool.tile([P, PER_BANK, P], F32)
                for q in range(PER_BANK):
                    first = (PER_BANK * m + q) * P
                    nc.tensor.transpose(turned[:, q, :], pairs[:, first : first + P], ident_f32[:])
                turned_in[r].append(turned)

        def regroup(r):
            lined = grouped_pool.tile([P, DEPTH], BF16, align_bytes=64)
            lined_pairs = lined[:].bitcast(F32).rearrange("p (g c u) -> p g c u", g=PASSES, u=2)
            for m in range(BANKS):
                source = turned_in[r][m][:].rearrange("p (g u) c -> p g c u", u=2)
                target = lined_pairs[:, 2 * m : 2 * m + 2, :, :]
                if r >= FIRST_SHARED and m > 0:
                    nc.scalar.copy(out=target, in_=source)
                else:
                    nc.vector.tensor_copy(out=target, in_=source)
            grouped[r] = lined

        def quantise(r):
            if r < X_TILES:
                cols = slice(r * P, (r + 1) * P)
                for g in range(PASSES):
                    nc.vector.quantize_mx(
                        out=x_codes[:, g, cols].bitcast(FP8X4),
                        scales=x_scales[:, g, cols],
                        in_=grouped[r][:, g * K_PASS : (g + 1) * K_PASS],
                    )
            else:
                w_codes = weight_pool.tile([P, PASSES * P], U32, align_bytes=64)
                w_scales = weight_pool.tile([P, PASSES * P], U8, align_bytes=64)
                for first, width in ((0, 4 * P), (4 * P, 2 * P)):
                    nc.vector.quantize_mx(
                        out=w_codes[:, first : first + width].bitcast(FP8X4),
                        scales=w_scales[:, first : first + width],
                        in_=grouped[r][:, PACK * first : PACK * (first + width)],
                    )
                weights[r - X_TILES] = (w_codes, w_scales)

        def multiply(j):
            w_codes, w_scales = weights[j]
            sums[j] = []
            for h in range(HALVES):
                half = slice(h * N_MOVE, (h + 1) * N_MOVE)
                acc = acc_pool.tile([P, N_MOVE], F32)
                for g in range(PASSES):
                    w_cols = slice(g * P, (g + 1) * P)
                    nc.tensor.matmul_mx(
                        out=acc[:],
                        lhsT=w_codes[:, w_cols].bitcast(FP8X4),
                        lhsT_scale=w_scales[:, w_cols],
                        rhs=x_codes[:, g, half].bitcast(FP8X4),
                        rhs_scale=x_scales[:, g, half],
                        start=(g == 0),
                        stop=(g == PASSES - 1),
                    )
                sums[j].append(acc)

        def clip(j, h):
            if h == 0:
                sim = sim_pool.tile([P, BATCH], F32)
                sims[j] = sim
            half_cols = slice(h * N_MOVE, (h + 1) * N_MOVE)
            nc.vector.tensor_scalar(
                out=sims[j][:, half_cols], in0=sums[j][h][:], scalar1=0.0, scalar2=1.0,
                op0=ALU.max, op1=ALU.min,
            )

        def count(j, h):
            if h == 0:
                stats = small.tile([P, HALVES, 6], F32)
                counts[j] = stats
            nc.vector.bn_stats(
                out=counts[j][:, h, :], in_=sims[j][:, h * N_MOVE : (h + 1) * N_MOVE]
            )

        def fit(j):
            mean_var = small.tile([P, 2], F32)
            nc.vector.bn_aggr(out=mean_var[:], in_=counts[j][:].rearrange("p h s -> p (h s)"))
            padded_var = small.tile([P, 1], F32)
            nc.gpsimd.tensor_scalar(
                out=padded_var[:], in0=mean_var[:, 1:2], scalar1=BN_EPS, scalar2=1.0,
                op0=ALU.add, op1=ALU.mult,
            )
            inverse_std = small.tile([P, 1], F32)
            nc.gpsimd.tensor_tensor(
                out=inverse_std[:], in0=padded_var[:], in1=power_minus_half[:], op=ALU.pow
            )
            slope = small.tile([P, 1], F32)
            nc.gpsimd.tensor_tensor(
                out=slope[:], in0=inverse_std[:], in1=gain_shift[:, j : j + 1], op=ALU.mult
            )
            drop = small.tile([P, 1], F32)
            nc.gpsimd.tensor_scalar(
                out=drop[:], in0=mean_var[:, 0:1], scalar1=slope[:, 0:1],
                scalar2=gain_shift[:, W_TILES + j : W_TILES + j + 1],
                op0=ALU.mult, op1=ALU.add,
            )
            lines[j] = (slope, drop)

        def normalise(j):
            slope, drop = lines[j]
            normed = normed_pool.tile([P, BATCH], F32)
            for h in range(HALVES):
                half_cols = slice(h * N_MOVE, (h + 1) * N_MOVE)
                nc.vector.tensor_scalar(
                    out=normed[:, half_cols], in0=sims[j][:, half_cols],
                    scalar1=slope[:, 0:1], scalar2=drop[:, 0:1],
                    op0=ALU.mult, op1=ALU.subtract,
                )
            normeds[j] = normed

        def turn_back(j):
            turned_out[j] = []
            for m in range(X_TILES // PER_BANK):
                turned_back = turn_out_pool.tile([P, PER_BANK, P], F32)
                for q in range(PER_BANK):
                    t = PER_BANK * m + q
                    nc.tensor.transpose(
                        turned_back[:, q, :], normeds[j][:, t * P : (t + 1) * P], ident_f32[:]
                    )
                turned_out[j].append(turned_back)

        def store(j):
            for m in range(X_TILES // PER_BANK):
                result = result_pool.tile([P, PER_BANK, P], F32)
                nc.scalar.copy(out=result[:], in_=turned_out[j][m][:])
                nc.sync.dma_start(
                    out=out_tiles[j][:, PER_BANK * m : PER_BANK * (m + 1), :], in_=result[:]
                )

        for r in range(LOADS_AHEAD):
            load(r)
        load_gain_and_shift()
        for step in range(ROW_TILES + 6):
            scaled_now = step - 1
            grouped_now = step - 2
            multiplied_now = step - 3 - X_TILES
            fitted_now = step - 4 - X_TILES
            stored_now = step - 5 - X_TILES
            if 0 <= multiplied_now < W_TILES:
                multiply(multiplied_now)
            if 0 <= fitted_now < W_TILES:
                count(fitted_now, 1)
            if 0 <= stored_now < W_TILES:
                normalise(stored_now)
                turn_back(stored_now)
            if 0 <= fitted_now < W_TILES:
                fit(fitted_now)
            if 0 <= scaled_now < ROW_TILES:
                scale(scaled_now)
            if 0 <= grouped_now < ROW_TILES:
                regroup(grouped_now)
            if 0 <= scaled_now < ROW_TILES:
                turn(scaled_now)
            if 0 <= multiplied_now < W_TILES:
                clip(multiplied_now, 0)
            if 0 <= grouped_now < ROW_TILES:
                quantise(grouped_now)
            if 0 <= multiplied_now < W_TILES:
                clip(multiplied_now, 1)
            if step < ROW_TILES:
                measure(step)
            if 0 <= multiplied_now < W_TILES:
                count(multiplied_now, 0)
            if 0 <= stored_now < W_TILES:
                store(stored_now)
            if step + LOADS_AHEAD < ROW_TILES:
                load(step + LOADS_AHEAD)
            if step == X_TILES:
                spread_gain_and_shift()
